import numpy as np
import ml_dtypes


def mxq(x, axis, fmt="e4m3"):
    dtype, down = {"e4m3": (ml_dtypes.float8_e4m3fn, 7), "e5m2": (ml_dtypes.float8_e5m2, 14)}[fmt]
    v = np.moveaxis(np.asarray(x, np.float32).astype(ml_dtypes.bfloat16).astype(np.float64), axis, -1)
    blocks = v.reshape(v.shape[:-1] + (-1, 32))
    amax = np.abs(blocks).max(-1, keepdims=True)
    byte = np.maximum(np.where(amax > 0, np.frexp(amax)[1] - 1 + 127, 0) - down, 1)
    scale = np.exp2(byte - 127.0)
    codes = (blocks / scale).astype(np.float32).astype(dtype).astype(np.float64)
    return np.moveaxis((codes * scale).reshape(v.shape), -1, axis)


WIDE = False


def mx_kscale(k):
    if not WIDE:
        return np.ones(k)
    levels = np.array([10, -10, 5, -5, 0])
    a = np.random.permutation(np.resize(levels, k // 512 * 4)).reshape(k // 512, 4)
    idx = np.arange(k)
    return np.exp2(a[idx // 512, idx % 128 // 32])


BF16 = ml_dtypes.bfloat16


def bf(x):
    return np.asarray(x, np.float32).astype(BF16)


def f64(x):
    return np.asarray(x).astype(np.float64)


B, H, E, V = 128, 512, 512, 128


def sigmoid(v):
    return 1.0 / (1.0 + np.exp(-v))


def setup_inputs():
    s, t = mx_kscale(E), mx_kscale(H)
    return {
        "input_data": bf(np.random.standard_normal((B, E)) * s),
        "previous_hidden_state": bf(np.random.standard_normal((B, H)) * t),
        "c_t": bf(np.random.standard_normal((B, H)) * 0.7),
        "w_ip_o": bf(np.random.standard_normal((E, H)) / np.sqrt(E) / s[:, None]),
        "w_output": bf(np.random.standard_normal((H, H)) / np.sqrt(H) / t[:, None]),
        "w_output_c": bf(np.random.standard_normal((H, H)) / np.sqrt(H)),
        "w_op": bf(np.random.standard_normal((H, V)) * 3.0 / np.sqrt(H)),
    }


def reference(input_data, previous_hidden_state, c_t, w_ip_o, w_output, w_output_c, w_op):
    ct = f64(c_t)
    zo = (mxq(f64(input_data), 1, "e4m3") @ mxq(f64(w_ip_o), 0, "e4m3")) \
        + (mxq(f64(previous_hidden_state), 1, "e4m3") @ mxq(f64(w_output), 0, "e4m3"))
    ot = sigmoid(zo + (mxq(ct, 1, "e4m3") @ mxq(f64(w_output_c), 0, "e4m3")))
    ht = ot * np.tanh(ct)
    yt = sigmoid(mxq(ht, 1, "e4m3") @ mxq(f64(w_op), 0, "e4m3"))
    return yt, ht

@@ -1,0 +1,178 @@
+import concourse.mybir as mybir
+from concourse.masks import make_identity
+
+F32 = mybir.dt.float32
+BF16 = mybir.dt.bfloat16
+U32 = mybir.dt.uint32
+U8 = mybir.dt.uint8
+FP8X4 = mybir.dt.float8_e4m3fn_x4
+SIGMOID = mybir.ActivationFunctionType.Sigmoid
+TANH = mybir.ActivationFunctionType.Tanh
+
+P = 128
+PACK = 4
+K = P * PACK
+BATCH = 128
+HIDDEN = 512
+READOUT = 128
+H_TILES = HIDDEN // P
+HALF = HIDDEN // 2
+RUN = 4
+
+FLOPS = 2 * BATCH * K * (3 * HIDDEN + READOUT)
+
+
+def regroup(copy, grouped, raw):
+    copy(
+        out=grouped.rearrange("p (c i) t -> p c t i", i=RUN),
+        in_=raw.rearrange("p t (c i) -> p c t i", i=RUN),
+    )
+
+
+def tile_lstm_peephole_build_pb_s_kernel(
+    tc, input_data, previous_hidden_state, c_t, w_ip_o, w_output, w_output_c, w_op, out_0, out_1
+):
+    nc = tc.nc
+    acts = [c_t, input_data, previous_hidden_state]
+    weights = [w_output_c, w_ip_o, w_output]
+    terms = len(acts)
+
+    with tc.tile_pool(name="sbuf", bufs=1) as sbuf, tc.psum_pool(name="psum", bufs=1) as psum, tc.manual_schedule():
+        ident = sbuf.tile([P, P], F32, name="ident")
+        warm_in = sbuf.tile([P, 1], F32, name="warm_in")
+        warm_out = sbuf.tile([P, 1], F32, name="warm_out")
+        act_raw = [sbuf.tile([BATCH, K], BF16, name="act_raw%d" % a) for a in range(terms)]
+        act_grouped = [
+            sbuf.tile([P, BATCH * PACK], BF16, name="act_grouped%d" % a, align_bytes=64) for a in range(terms)
+        ]
+        act_codes = sbuf.tile([P, terms, BATCH], U32, name="act_codes", align_bytes=64)
+        act_scales = sbuf.tile([P, terms, BATCH], U8, name="act_scales", align_bytes=64)
+        w_raw = [sbuf.tile([P, PACK, HIDDEN], BF16, name="w_raw%d" % w) for w in range(terms)]
+        w_grouped = [sbuf.tile([P, HIDDEN, PACK], BF16, name="w_grouped%d" % w, align_bytes=64) for w in range(terms)]
+        w_codes = sbuf.tile([P, terms, HIDDEN], U32, name="w_codes", align_bytes=64)
+        w_scales = sbuf.tile([P, terms, HIDDEN], U8, name="w_scales", align_bytes=64)
+        wop_raw = sbuf.tile([P, PACK, READOUT], BF16, name="wop_raw")
+        wop_grouped = sbuf.tile([P, READOUT, PACK], BF16, name="wop_grouped", align_bytes=64)
+        wop_codes = sbuf.tile([P, READOUT], U32, name="wop_codes", align_bytes=64)
+        wop_scales = sbuf.tile([P, READOUT], U8, name="wop_scales", align_bytes=64)
+        tanh_c = sbuf.tile([BATCH, HIDDEN], F32, name="tanh_c")
+        gate = sbuf.tile([BATCH, HIDDEN], F32, name="gate")
+        hidden = sbuf.tile([BATCH, HIDDEN], F32, name="hidden")
+        gate_t = sbuf.tile([P, H_TILES, BATCH], F32, name="gate_t")
+        hid_grouped = sbuf.tile([P, BATCH, PACK], BF16, name="hid_grouped", align_bytes=64)
+        hid_codes = sbuf.tile([P, BATCH], U32, name="hid_codes", align_bytes=64)
+        hid_scales = sbuf.tile([P, BATCH], U8, name="hid_scales", align_bytes=64)
+        readout = sbuf.tile([BATCH, READOUT], F32, name="readout")
+
+        act_t = [psum.tile([P, 2, BATCH], F32, name="act_t%d" % a, tag="bank%d" % a) for a in range(terms)]
+        tanh_t = psum.tile([P, H_TILES, BATCH], F32, name="tanh_t", tag="bank3")
+        z_t = [psum.tile([P, BATCH], F32, name="z_t%d" % j, tag="bank%d" % (4 + j)) for j in range(H_TILES)]
+
+        make_identity(nc, ident[:])
+        nc.vector.memset(warm_in[:], 0.0)
+        nc.scalar.activation(out=warm_out[:], in_=warm_in[:], func=SIGMOID)
+
+        for a in range(terms):
+            nc.sync.dma_start(out=act_raw[a][:], in_=acts[a])
+        for w in range(terms):
+            nc.sync.dma_start(out=w_raw[w][:], in_=weights[w].rearrange("(p t) n -> p t n", t=PACK))
+        nc.sync.dma_start(out=wop_raw[:], in_=w_op.rearrange("(t p) v -> p t v", p=P))
+
+        nc.scalar.activation(out=tanh_c[:], in_=act_raw[0][:], func=TANH)
+        for a in range(terms):
+            words = act_raw[a][:].bitcast(F32).rearrange("b (p u) -> b u p", u=2)
+            for u in range(2):
+                nc.tensor.transpose(out=act_t[a][:, u, :], in_=words[:, u, :], identity=ident[:])
+        for j in range(H_TILES):
+            nc.tensor.transpose(out=tanh_t[:, j, :], in_=tanh_c[:, j * P : (j + 1) * P], identity=ident[:])
+        for a in range(terms):
+            copy = nc.vector.tensor_copy if a == 0 else nc.scalar.copy
+            copy(
+                out=act_grouped[a][:].bitcast(F32).rearrange("p (b u) -> p b u", u=2),
+                in_=act_t[a][:].rearrange("p u b -> p b u"),
+            )
+        for a in range(terms):
+            nc.vector.quantize_mx(
+                out=act_codes[:, a, :].bitcast(FP8X4), scales=act_scales[:, a, :], in_=act_grouped[a][:]
+            )
+
+        z = psum.tile([BATCH, HIDDEN], F32, name="z", tag="bank0")
+
+        def quantise_half(w, half):
+            cols = slice(half * HALF, (half + 1) * HALF)
+            nc.vector.quantize_mx(
+                out=w_codes[:, w, cols].bitcast(FP8X4),
+                scales=w_scales[:, w, cols],
+                in_=w_grouped[w][:, cols, :].rearrange("p n t -> p (n t)"),
+            )
+
+        def transposed_gate_passes(w, half):
+            for j in range(half * H_TILES // 2, (half + 1) * H_TILES // 2):
+                cols = slice(j * P, (j + 1) * P)
+                nc.tensor.matmul_mx(
+                    out=z_t[j][:],
+                    lhsT=w_codes[:, w, cols].bitcast(FP8X4),
+                    lhsT_scale=w_scales[:, w, cols],
+                    rhs=act_codes[:, w, :].bitcast(FP8X4),
+                    rhs_scale=act_scales[:, w, :],
+                    start=(w == 0),
+                    stop=(w == terms - 1),
+                )
+
+        def gate_pass(w):
+            nc.tensor.matmul_mx(
+                out=z[:],
+                lhsT=act_codes[:, w, :].bitcast(FP8X4),
+                lhsT_scale=act_scales[:, w, :],
+                rhs=w_codes[:, w, :].bitcast(FP8X4),
+                rhs_scale=w_scales[:, w, :],
+                start=(w == 0),
+                stop=(w == terms - 1),
+            )
+
+        def second_half(w):
+            quantise_half(w, 1)
+            transposed_gate_passes(w, 1)
+            gate_pass(w)
+
+        for w in range(terms):
+            regroup(nc.vector.tensor_copy, w_grouped[w][:, :HALF, :], w_raw[w][:, :, :HALF])
+            regroup(nc.scalar.copy, w_grouped[w][:, HALF:, :], w_raw[w][:, :, HALF:])
+            if w > 0:
+                second_half(w - 1)
+            quantise_half(w, 0)
+            transposed_gate_passes(w, 0)
+        regroup(nc.vector.tensor_copy, wop_grouped[:], wop_raw[:])
+        second_half(terms - 1)
+        nc.vector.quantize_mx(
+            out=wop_codes[:].bitcast(FP8X4), scales=wop_scales[:], in_=wop_grouped[:].rearrange("p v t -> p (v t)")
+        )
+
+        for j in range(H_TILES):
+            nc.scalar.activation(out=gate_t[:, j, :], in_=z_t[j][:], func=SIGMOID)
+        nc.vector.tensor_tensor(
+            out=hid_grouped[:],
+            in0=gate_t[:].rearrange("p t b -> p b t"),
+            in1=tanh_t[:].rearrange("p t b -> p b t"),
+            op=mybir.AluOpType.mult,
+        )
+        nc.vector.quantize_mx(
+            out=hid_codes[:].bitcast(FP8X4), scales=hid_scales[:], in_=hid_grouped[:].rearrange("p b t -> p (b t)")
+        )
+        y = psum.tile([BATCH, READOUT], F32, name="y", tag="bank1")
+        nc.tensor.matmul_mx(
+            out=y[:],
+            lhsT=hid_codes[:].bitcast(FP8X4),
+            lhsT_scale=hid_scales[:],
+            rhs=wop_codes[:].bitcast(FP8X4),
+            rhs_scale=wop_scales[:],
+            start=True,
+            stop=True,
+        )
+
+        nc.scalar.activation(out=gate[:], in_=z[:], func=SIGMOID)
+        nc.vector.tensor_tensor(out=hidden[:], in0=gate[:], in1=tanh_c[:], op=mybir.AluOpType.mult)
+        nc.sync.dma_start(out=out_1, in_=hidden[:])
+
+        nc.scalar.activation(out=readout[:], in_=y[:], func=SIGMOID)
+        nc.sync.dma_start(out=out_0, in_=readout[:])

@@ -98,28 +98,27 @@ def tile_lstm_peephole_build_pb_s_kernel(
 
         z = psum.tile([BATCH, HIDDEN], F32, name="z", tag="bank0")
 
-        def quantise_half(w, half):
-            cols = slice(half * HALF, (half + 1) * HALF)
+        def quantise_tiles(w, first, count):
+            cols = slice(first * P, (first + count) * P)
             nc.vector.quantize_mx(
                 out=w_codes[:, w, cols].bitcast(FP8X4),
                 scales=w_scales[:, w, cols],
                 in_=w_grouped[w][:, cols, :].rearrange("p n t -> p (n t)"),
             )
-
-        def transposed_gate_passes(w, half):
-            for j in range(half * H_TILES // 2, (half + 1) * H_TILES // 2):
-                cols = slice(j * P, (j + 1) * P)
+            for j in range(first, first + count):
+                tile_cols = slice(j * P, (j + 1) * P)
                 nc.tensor.matmul_mx(
                     out=z_t[j][:],
-                    lhsT=w_codes[:, w, cols].bitcast(FP8X4),
-                    lhsT_scale=w_scales[:, w, cols],
+                    lhsT=w_codes[:, w, tile_cols].bitcast(FP8X4),
+                    lhsT_scale=w_scales[:, w, tile_cols],
                     rhs=act_codes[:, w, :].bitcast(FP8X4),
                     rhs_scale=act_scales[:, w, :],
                     start=(w == 0),
                     stop=(w == terms - 1),
                 )
 
-        def gate_pass(w):
+        def last_tile(w):
+            quantise_tiles(w, H_TILES - 1, 1)
             nc.tensor.matmul_mx(
                 out=z[:],
                 lhsT=act_codes[:, w, :].bitcast(FP8X4),
@@ -130,20 +129,17 @@ def tile_lstm_peephole_build_pb_s_kernel(
                 stop=(w == terms - 1),
             )
 
-        def second_half(w):
-            quantise_half(w, 1)
-            transposed_gate_passes(w, 1)
-            gate_pass(w)
-
         for w in range(terms):
             regroup(nc.vector.tensor_copy, w_grouped[w][:, :HALF, :], w_raw[w][:, :, :HALF])
-            regroup(nc.scalar.copy, w_grouped[w][:, HALF:, :], w_raw[w][:, :, HALF:])
+            for j in range(H_TILES // 2, H_TILES):
+                tile_cols = slice(j * P, (j + 1) * P)
+                regroup(nc.scalar.copy, w_grouped[w][:, tile_cols, :], w_raw[w][:, :, tile_cols])
             if w > 0:
-                second_half(w - 1)
-            quantise_half(w, 0)
-            transposed_gate_passes(w, 0)
+                last_tile(w - 1)
+            quantise_tiles(w, 0, H_TILES // 2)
+            quantise_tiles(w, H_TILES // 2, 1)
+        last_tile(terms - 1)
         regroup(nc.vector.tensor_copy, wop_grouped[:], wop_raw[:])
-        second_half(terms - 1)
         nc.vector.quantize_mx(
             out=wop_codes[:].bitcast(FP8X4), scales=wop_scales[:], in_=wop_grouped[:].rearrange("p v t -> p (v t)")
         )

@@ -72,53 +72,57 @@ def tile_lstm_peephole_build_pb_s_kernel(
         nc.vector.memset(warm_in[:], 0.0)
         nc.scalar.activation(out=warm_out[:], in_=warm_in[:], func=SIGMOID)
 
-        for a in range(terms):
-            nc.sync.dma_start(out=act_raw[a][:], in_=acts[a])
         for w in range(terms):
+            nc.sync.dma_start(out=act_raw[w][:], in_=acts[w])
             nc.sync.dma_start(out=w_raw[w][:], in_=weights[w].rearrange("(p t) n -> p t n", t=PACK))
         nc.sync.dma_start(out=wop_raw[:], in_=w_op.rearrange("(t p) v -> p t v", p=P))
 
-        nc.scalar.activation(out=tanh_c[:], in_=act_raw[0][:], func=TANH)
-        for a in range(terms):
+        def transpose_words(a):
             words = act_raw[a][:].bitcast(F32).rearrange("b (p u) -> b u p", u=2)
             for u in range(2):
                 nc.tensor.transpose(out=act_t[a][:, u, :], in_=words[:, u, :], identity=ident[:])
-        for j in range(H_TILES):
-            nc.tensor.transpose(out=tanh_t[:, j, :], in_=tanh_c[:, j * P : (j + 1) * P], identity=ident[:])
-        for a in range(terms):
-            copy = nc.vector.tensor_copy if a == 0 else nc.scalar.copy
-            copy(
+
+        def group_words(a):
+            nc.scalar.copy(
                 out=act_grouped[a][:].bitcast(F32).rearrange("p (b u) -> p b u", u=2),
                 in_=act_t[a][:].rearrange("p u b -> p b u"),
             )
-        for a in range(terms):
+
+        def quantise_act(a):
             nc.vector.quantize_mx(
                 out=act_codes[:, a, :].bitcast(FP8X4), scales=act_scales[:, a, :], in_=act_grouped[a][:]
             )
 
+        nc.scalar.activation(out=tanh_c[:], in_=act_raw[0][:], func=TANH)
+        transpose_words(0)
+        for j in range(H_TILES):
+            nc.tensor.transpose(out=tanh_t[:, j, :], in_=tanh_c[:, j * P : (j + 1) * P], identity=ident[:])
+        group_words(0)
+
         z = psum.tile([BATCH, HIDDEN], F32, name="z", tag="bank0")
 
-        def quantise_tiles(w, first, count):
-            cols = slice(first * P, (first + count) * P)
+        def quantise_half(w, half):
+            cols = slice(half * HALF, (half + 1) * HALF)
             nc.vector.quantize_mx(
                 out=w_codes[:, w, cols].bitcast(FP8X4),
                 scales=w_scales[:, w, cols],
                 in_=w_grouped[w][:, cols, :].rearrange("p n t -> p (n t)"),
             )
-            for j in range(first, first + count):
-                tile_cols = slice(j * P, (j + 1) * P)
+
+        def transposed_gate_passes(w, half):
+            for j in range(half * H_TILES // 2, (half + 1) * H_TILES // 2):
+                cols = slice(j * P, (j + 1) * P)
                 nc.tensor.matmul_mx(
                     out=z_t[j][:],
-                    lhsT=w_codes[:, w, tile_cols].bitcast(FP8X4),
-                    lhsT_scale=w_scales[:, w, tile_cols],
+                    lhsT=w_codes[:, w, cols].bitcast(FP8X4),
+                    lhsT_scale=w_scales[:, w, cols],
                     rhs=act_codes[:, w, :].bitcast(FP8X4),
                     rhs_scale=act_scales[:, w, :],
                     start=(w == 0),
                     stop=(w == terms - 1),
                 )
 
-        def last_tile(w):
-            quantise_tiles(w, H_TILES - 1, 1)
+        def gate_pass(w):
             nc.tensor.matmul_mx(
                 out=z[:],
                 lhsT=act_codes[:, w, :].bitcast(FP8X4),
@@ -129,16 +133,24 @@ def tile_lstm_peephole_build_pb_s_kernel(
                 stop=(w == terms - 1),
             )
 
+        def second_half(w):
+            quantise_half(w, 1)
+            transposed_gate_passes(w, 1)
+            gate_pass(w)
+
         for w in range(terms):
+            if w + 1 < terms:
+                transpose_words(w + 1)
             regroup(nc.vector.tensor_copy, w_grouped[w][:, :HALF, :], w_raw[w][:, :, :HALF])
-            for j in range(H_TILES // 2, H_TILES):
-                tile_cols = slice(j * P, (j + 1) * P)
-                regroup(nc.scalar.copy, w_grouped[w][:, tile_cols, :], w_raw[w][:, :, tile_cols])
+            regroup(nc.scalar.copy, w_grouped[w][:, HALF:, :], w_raw[w][:, :, HALF:])
+            if w + 1 < terms:
+                group_words(w + 1)
             if w > 0:
-                last_tile(w - 1)
-            quantise_tiles(w, 0, H_TILES // 2)
-            quantise_tiles(w, H_TILES // 2, 1)
-        last_tile(terms - 1)
+                second_half(w - 1)
+            quantise_act(w)
+            quantise_half(w, 0)
+            transposed_gate_passes(w, 0)
+        second_half(terms - 1)
         regroup(nc.vector.tensor_copy, wop_grouped[:], wop_raw[:])
         nc.vector.quantize_mx(
             out=wop_codes[:].bitcast(FP8X4), scales=wop_scales[:], in_=wop_grouped[:].rearrange("p v t -> p (v t)")

@@ -178,9 +178,13 @@ def tile_lstm_peephole_build_pb_s_kernel(
             stop=True,
         )
 
-        nc.scalar.activation(out=gate[:], in_=z[:], func=SIGMOID)
-        nc.vector.tensor_tensor(out=hidden[:], in0=gate[:], in1=tanh_c[:], op=mybir.AluOpType.mult)
-        nc.sync.dma_start(out=out_1, in_=hidden[:])
+        for half in range(2):
+            cols = slice(half * HALF, (half + 1) * HALF)
+            nc.scalar.activation(out=gate[:, cols], in_=z[:, cols], func=SIGMOID)
+        for half in range(2):
+            cols = slice(half * HALF, (half + 1) * HALF)
+            nc.vector.tensor_tensor(out=hidden[:, cols], in0=gate[:, cols], in1=tanh_c[:, cols], op=mybir.AluOpType.mult)
+            nc.sync.dma_start(out=out_1[:, cols], in_=hidden[:, cols])
 
         nc.scalar.activation(out=readout[:], in_=y[:], func=SIGMOID)
         nc.sync.dma_start(out=out_0, in_=readout[:])

@@ -164,6 +164,16 @@ def tile_lstm_peephole_build_pb_s_kernel(
             in1=tanh_t[:].rearrange("p t b -> p b t"),
             op=mybir.AluOpType.mult,
         )
+
+        def returned_half(half):
+            cols = slice(half * HALF, (half + 1) * HALF)
+            nc.vector.tensor_tensor(out=hidden[:, cols], in0=gate[:, cols], in1=tanh_c[:, cols], op=mybir.AluOpType.mult)
+            nc.sync.dma_start(out=out_1[:, cols], in_=hidden[:, cols])
+
+        for half in range(2):
+            cols = slice(half * HALF, (half + 1) * HALF)
+            nc.scalar.activation(out=gate[:, cols], in_=z[:, cols], func=SIGMOID)
+        returned_half(0)
         nc.vector.quantize_mx(
             out=hid_codes[:].bitcast(FP8X4), scales=hid_scales[:], in_=hid_grouped[:].rearrange("p b t -> p (b t)")
         )
@@ -177,14 +187,7 @@ def tile_lstm_peephole_build_pb_s_kernel(
             start=True,
             stop=True,
         )
-
-        for half in range(2):
-            cols = slice(half * HALF, (half + 1) * HALF)
-            nc.scalar.activation(out=gate[:, cols], in_=z[:, cols], func=SIGMOID)
-        for half in range(2):
-            cols = slice(half * HALF, (half + 1) * HALF)
-            nc.vector.tensor_tensor(out=hidden[:, cols], in0=gate[:, cols], in1=tanh_c[:, cols], op=mybir.AluOpType.mult)
-            nc.sync.dma_start(out=out_1[:, cols], in_=hidden[:, cols])
+        returned_half(1)
 
         nc.scalar.activation(out=readout[:], in_=y[:], func=SIGMOID)
         nc.sync.dma_start(out=out_0, in_=readout[:])

@@ -138,11 +138,35 @@ def tile_lstm_peephole_build_pb_s_kernel(
             transposed_gate_passes(w, 1)
             gate_pass(w)
 
+        def quantise_tile(w, j):
+            cols = slice(j * P, (j + 1) * P)
+            nc.vector.quantize_mx(
+                out=w_codes[:, w, cols].bitcast(FP8X4),
+                scales=w_scales[:, w, cols],
+                in_=w_grouped[w][:, cols, :].rearrange("p n t -> p (n t)"),
+            )
+
+        def transposed_gate_pass(w, j):
+            cols = slice(j * P, (j + 1) * P)
+            nc.tensor.matmul_mx(
+                out=z_t[j][:],
+                lhsT=w_codes[:, w, cols].bitcast(FP8X4),
+                lhsT_scale=w_scales[:, w, cols],
+                rhs=act_codes[:, w, :].bitcast(FP8X4),
+                rhs_scale=act_scales[:, w, :],
+                start=(w == 0),
+                stop=(w == terms - 1),
+            )
+
         for w in range(terms):
             if w + 1 < terms:
                 transpose_words(w + 1)
             regroup(nc.vector.tensor_copy, w_grouped[w][:, :HALF, :], w_raw[w][:, :, :HALF])
-            regroup(nc.scalar.copy, w_grouped[w][:, HALF:, :], w_raw[w][:, :, HALF:])
+            if w + 1 < terms:
+                regroup(nc.scalar.copy, w_grouped[w][:, HALF:, :], w_raw[w][:, :, HALF:])
+            else:
+                for j in range(H_TILES // 2, H_TILES):
+                    regroup(nc.scalar.copy, w_grouped[w][:, j * P : (j + 1) * P, :], w_raw[w][:, :, j * P : (j + 1) * P])
             if w + 1 < terms:
                 group_words(w + 1)
             if w > 0:
@@ -150,7 +174,10 @@ def tile_lstm_peephole_build_pb_s_kernel(
             quantise_act(w)
             quantise_half(w, 0)
             transposed_gate_passes(w, 0)
-        second_half(terms - 1)
+        for j in range(H_TILES // 2, H_TILES):
+            quantise_tile(terms - 1, j)
+            transposed_gate_pass(terms - 1, j)
+        gate_pass(terms - 1)
         regroup(nc.vector.tensor_copy, wop_grouped[:], wop_raw[:])
         nc.vector.quantize_mx(
             out=wop_codes[:].bitcast(FP8X4), scales=wop_scales[:], in_=wop_grouped[:].rearrange("p v t -> p (v t)")

@@ -17,6 +17,7 @@ HIDDEN = 512
 READOUT = 128
 H_TILES = HIDDEN // P
 HALF = HIDDEN // 2
+V_COLS = 224
 RUN = 4
 
 FLOPS = 2 * BATCH * K * (3 * HIDDEN + READOUT)
@@ -161,7 +162,8 @@ def tile_lstm_peephole_build_pb_s_kernel(
         for w in range(terms):
             if w + 1 < terms:
                 transpose_words(w + 1)
-            regroup(nc.vector.tensor_copy, w_grouped[w][:, :HALF, :], w_raw[w][:, :, :HALF])
+            regroup(nc.vector.tensor_copy, w_grouped[w][:, :V_COLS, :], w_raw[w][:, :, :V_COLS])
+            regroup(nc.scalar.copy, w_grouped[w][:, V_COLS:HALF, :], w_raw[w][:, :, V_COLS:HALF])
             if w + 1 < terms:
                 regroup(nc.scalar.copy, w_grouped[w][:, HALF:, :], w_raw[w][:, :, HALF:])
             else:

@@ -17,7 +17,7 @@ HIDDEN = 512
 READOUT = 128
 H_TILES = HIDDEN // P
 HALF = HIDDEN // 2
-V_COLS = 224
+V_COLS = 240
 RUN = 4
 
 FLOPS = 2 * BATCH * K * (3 * HIDDEN + READOUT)

import concourse.mybir as mybir
from concourse.masks import make_identity

F32 = mybir.dt.float32
BF16 = mybir.dt.bfloat16
U32 = mybir.dt.uint32
U8 = mybir.dt.uint8
FP8X4 = mybir.dt.float8_e4m3fn_x4
SIGMOID = mybir.ActivationFunctionType.Sigmoid
TANH = mybir.ActivationFunctionType.Tanh

P = 128
PACK = 4
K = P * PACK
BATCH = 128
HIDDEN = 512
READOUT = 128
H_TILES = HIDDEN // P
HALF = HIDDEN // 2
V_COLS = 240
RUN = 4

FLOPS = 2 * BATCH * K * (3 * HIDDEN + READOUT)


def regroup(copy, grouped, raw):
    copy(
        out=grouped.rearrange("p (c i) t -> p c t i", i=RUN),
        in_=raw.rearrange("p t (c i) -> p c t i", i=RUN),
    )


def tile_lstm_peephole_build_pb_s_kernel(
    tc, input_data, previous_hidden_state, c_t, w_ip_o, w_output, w_output_c, w_op, out_0, out_1
):
    nc = tc.nc
    acts = [c_t, input_data, previous_hidden_state]
    weights = [w_output_c, w_ip_o, w_output]
    terms = len(acts)

    with tc.tile_pool(name="sbuf", bufs=1) as sbuf, tc.psum_pool(name="psum", bufs=1) as psum, tc.manual_schedule():
        ident = sbuf.tile([P, P], F32, name="ident")
        warm_in = sbuf.tile([P, 1], F32, name="warm_in")
        warm_out = sbuf.tile([P, 1], F32, name="warm_out")
        act_raw = [sbuf.tile([BATCH, K], BF16, name="act_raw%d" % a) for a in range(terms)]
        act_grouped = [
            sbuf.tile([P, BATCH * PACK], BF16, name="act_grouped%d" % a, align_bytes=64) for a in range(terms)
        ]
        act_codes = sbuf.tile([P, terms, BATCH], U32, name="act_codes", align_bytes=64)
        act_scales = sbuf.tile([P, terms, BATCH], U8, name="act_scales", align_bytes=64)
        w_raw = [sbuf.tile([P, PACK, HIDDEN], BF16, name="w_raw%d" % w) for w in range(terms)]
        w_grouped = [sbuf.tile([P, HIDDEN, PACK], BF16, name="w_grouped%d" % w, align_bytes=64) for w in range(terms)]
        w_codes = sbuf.tile([P, terms, HIDDEN], U32, name="w_codes", align_bytes=64)
        w_scales = sbuf.tile([P, terms, HIDDEN], U8, name="w_scales", align_bytes=64)
        wop_raw = sbuf.tile([P, PACK, READOUT], BF16, name="wop_raw")
        wop_grouped = sbuf.tile([P, READOUT, PACK], BF16, name="wop_grouped", align_bytes=64)
        wop_codes = sbuf.tile([P, READOUT], U32, name="wop_codes", align_bytes=64)
        wop_scales = sbuf.tile([P, READOUT], U8, name="wop_scales", align_bytes=64)
        tanh_c = sbuf.tile([BATCH, HIDDEN], F32, name="tanh_c")
        gate = sbuf.tile([BATCH, HIDDEN], F32, name="gate")
        hidden = sbuf.tile([BATCH, HIDDEN], F32, name="hidden")
        gate_t = sbuf.tile([P, H_TILES, BATCH], F32, name="gate_t")
        hid_grouped = sbuf.tile([P, BATCH, PACK], BF16, name="hid_grouped", align_bytes=64)
        hid_codes = sbuf.tile([P, BATCH], U32, name="hid_codes", align_bytes=64)
        hid_scales = sbuf.tile([P, BATCH], U8, name="hid_scales", align_bytes=64)
        readout = sbuf.tile([BATCH, READOUT], F32, name="readout")

        act_t = [psum.tile([P, 2, BATCH], F32, name="act_t%d" % a, tag="bank%d" % a) for a in range(terms)]
        tanh_t = psum.tile([P, H_TILES, BATCH], F32, name="tanh_t", tag="bank3")
        z_t = [psum.tile([P, BATCH], F32, name="z_t%d" % j, tag="bank%d" % (4 + j)) for j in range(H_TILES)]

        make_identity(nc, ident[:])
        nc.vector.memset(warm_in[:], 0.0)
        nc.scalar.activation(out=warm_out[:], in_=warm_in[:], func=SIGMOID)

        for w in range(terms):
            nc.sync.dma_start(out=act_raw[w][:], in_=acts[w])
            nc.sync.dma_start(out=w_raw[w][:], in_=weights[w].rearrange("(p t) n -> p t n", t=PACK))
        nc.sync.dma_start(out=wop_raw[:], in_=w_op.rearrange("(t p) v -> p t v", p=P))

        def transpose_words(a):
            words = act_raw[a][:].bitcast(F32).rearrange("b (p u) -> b u p", u=2)
            for u in range(2):
                nc.tensor.transpose(out=act_t[a][:, u, :], in_=words[:, u, :], identity=ident[:])

        def group_words(a):
            nc.scalar.copy(
                out=act_grouped[a][:].bitcast(F32).rearrange("p (b u) -> p b u", u=2),
                in_=act_t[a][:].rearrange("p u b -> p b u"),
            )

        def quantise_act(a):
            nc.vector.quantize_mx(
                out=act_codes[:, a, :].bitcast(FP8X4), scales=act_scales[:, a, :], in_=act_grouped[a][:]
            )

        nc.scalar.activation(out=tanh_c[:], in_=act_raw[0][:], func=TANH)
        transpose_words(0)
        for j in range(H_TILES):
            nc.tensor.transpose(out=tanh_t[:, j, :], in_=tanh_c[:, j * P : (j + 1) * P], identity=ident[:])
        group_words(0)

        z = psum.tile([BATCH, HIDDEN], F32, name="z", tag="bank0")

        def quantise_half(w, half):
            cols = slice(half * HALF, (half + 1) * HALF)
            nc.vector.quantize_mx(
                out=w_codes[:, w, cols].bitcast(FP8X4),
                scales=w_scales[:, w, cols],
                in_=w_grouped[w][:, cols, :].rearrange("p n t -> p (n t)"),
            )

        def transposed_gate_passes(w, half):
            for j in range(half * H_TILES // 2, (half + 1) * H_TILES // 2):
                cols = slice(j * P, (j + 1) * P)
                nc.tensor.matmul_mx(
                    out=z_t[j][:],
                    lhsT=w_codes[:, w, cols].bitcast(FP8X4),
                    lhsT_scale=w_scales[:, w, cols],
                    rhs=act_codes[:, w, :].bitcast(FP8X4),
                    rhs_scale=act_scales[:, w, :],
                    start=(w == 0),
                    stop=(w == terms - 1),
                )

        def gate_pass(w):
            nc.tensor.matmul_mx(
                out=z[:],
                lhsT=act_codes[:, w, :].bitcast(FP8X4),
                lhsT_scale=act_scales[:, w, :],
                rhs=w_codes[:, w, :].bitcast(FP8X4),
                rhs_scale=w_scales[:, w, :],
                start=(w == 0),
                stop=(w == terms - 1),
            )

        def second_half(w):
            quantise_half(w, 1)
            transposed_gate_passes(w, 1)
            gate_pass(w)

        def quantise_tile(w, j):
            cols = slice(j * P, (j + 1) * P)
            nc.vector.quantize_mx(
                out=w_codes[:, w, cols].bitcast(FP8X4),
                scales=w_scales[:, w, cols],
                in_=w_grouped[w][:, cols, :].rearrange("p n t -> p (n t)"),
            )

        def transposed_gate_pass(w, j):
            cols = slice(j * P, (j + 1) * P)
            nc.tensor.matmul_mx(
                out=z_t[j][:],
                lhsT=w_codes[:, w, cols].bitcast(FP8X4),
                lhsT_scale=w_scales[:, w, cols],
                rhs=act_codes[:, w, :].bitcast(FP8X4),
                rhs_scale=act_scales[:, w, :],
                start=(w == 0),
                stop=(w == terms - 1),
            )

        for w in range(terms):
            if w + 1 < terms:
                transpose_words(w + 1)
            regroup(nc.vector.tensor_copy, w_grouped[w][:, :V_COLS, :], w_raw[w][:, :, :V_COLS])
            regroup(nc.scalar.copy, w_grouped[w][:, V_COLS:HALF, :], w_raw[w][:, :, V_COLS:HALF])
            if w + 1 < terms:
                regroup(nc.scalar.copy, w_grouped[w][:, HALF:, :], w_raw[w][:, :, HALF:])
            else:
                for j in range(H_TILES // 2, H_TILES):
                    regroup(nc.scalar.copy, w_grouped[w][:, j * P : (j + 1) * P, :], w_raw[w][:, :, j * P : (j + 1) * P])
            if w + 1 < terms:
                group_words(w + 1)
            if w > 0:
                second_half(w - 1)
            quantise_act(w)
            quantise_half(w, 0)
            transposed_gate_passes(w, 0)
        for j in range(H_TILES // 2, H_TILES):
            quantise_tile(terms - 1, j)
            transposed_gate_pass(terms - 1, j)
        gate_pass(terms - 1)
        regroup(nc.vector.tensor_copy, wop_grouped[:], wop_raw[:])
        nc.vector.quantize_mx(
            out=wop_codes[:].bitcast(FP8X4), scales=wop_scales[:], in_=wop_grouped[:].rearrange("p v t -> p (v t)")
        )

        for j in range(H_TILES):
            nc.scalar.activation(out=gate_t[:, j, :], in_=z_t[j][:], func=SIGMOID)
        nc.vector.tensor_tensor(
            out=hid_grouped[:],
            in0=gate_t[:].rearrange("p t b -> p b t"),
            in1=tanh_t[:].rearrange("p t b -> p b t"),
            op=mybir.AluOpType.mult,
        )

        def returned_half(half):
            cols = slice(half * HALF, (half + 1) * HALF)
            nc.vector.tensor_tensor(out=hidden[:, cols], in0=gate[:, cols], in1=tanh_c[:, cols], op=mybir.AluOpType.mult)
            nc.sync.dma_start(out=out_1[:, cols], in_=hidden[:, cols])

        for half in range(2):
            cols = slice(half * HALF, (half + 1) * HALF)
            nc.scalar.activation(out=gate[:, cols], in_=z[:, cols], func=SIGMOID)
        returned_half(0)
        nc.vector.quantize_mx(
            out=hid_codes[:].bitcast(FP8X4), scales=hid_scales[:], in_=hid_grouped[:].rearrange("p b t -> p (b t)")
        )
        y = psum.tile([BATCH, READOUT], F32, name="y", tag="bank1")
        nc.tensor.matmul_mx(
            out=y[:],
            lhsT=hid_codes[:].bitcast(FP8X4),
            lhsT_scale=hid_scales[:],
            rhs=wop_codes[:].bitcast(FP8X4),
            rhs_scale=wop_scales[:],
            start=True,
            stop=True,
        )
        returned_half(1)

        nc.scalar.activation(out=readout[:], in_=y[:], func=SIGMOID)
        nc.sync.dma_start(out=out_0, in_=readout[:])
